import numpy as np
import ml_dtypes


def mxq(x, axis, fmt="e4m3"):
    dtype, down = {"e4m3": (ml_dtypes.float8_e4m3fn, 7), "e5m2": (ml_dtypes.float8_e5m2, 14)}[fmt]
    v = np.moveaxis(np.asarray(x, np.float32).astype(ml_dtypes.bfloat16).astype(np.float64), axis, -1)
    blocks = v.reshape(v.shape[:-1] + (-1, 32))
    amax = np.abs(blocks).max(-1, keepdims=True)
    byte = np.maximum(np.where(amax > 0, np.frexp(amax)[1] - 1 + 127, 0) - down, 1)
    scale = np.exp2(byte - 127.0)
    codes = (blocks / scale).astype(np.float32).astype(dtype).astype(np.float64)
    return np.moveaxis((codes * scale).reshape(v.shape), -1, axis)


WIDE = False


def mx_kscale(k):
    if not WIDE:
        return np.ones(k)
    levels = np.array([10, -10, 5, -5, 0])
    a = np.random.permutation(np.resize(levels, k // 512 * 4)).reshape(k // 512, 4)
    idx = np.arange(k)
    return np.exp2(a[idx // 512, idx % 128 // 32])


BF16 = ml_dtypes.bfloat16


def bf(x):
    return np.asarray(x, np.float32).astype(BF16)


def f64(x):
    return np.asarray(x).astype(np.float64)


B, E, N = 512, 2048, 1024
CLIP_TANH = 10.0
DENS = 0.25


def setup_inputs():
    s, u = mx_kscale(E), mx_kscale(N)
    return {"x": bf(np.random.standard_normal((B, E)) * s),
            "llr": bf(np.random.standard_normal((B, N)) * u),
            "odd_weights": bf(np.random.standard_normal((E, E)) * 1.4 / np.sqrt(DENS * E) / s[:, None]),
            "llr_weights": bf(np.random.standard_normal((N, E)) * 1.4 / np.sqrt(DENS * N) / u[:, None]),
            "w_odd2even_mask": bf((np.random.random((E, E)) < DENS).astype(np.float64)),
            "w_skipconn2even_mask": bf((np.random.random((N, E)) < DENS).astype(np.float64))}


def reference(x, llr, odd_weights, llr_weights, w_odd2even_mask, w_skipconn2even_mask):
    msgs = mxq(f64(x), 1, "e4m3") @ mxq(f64(w_odd2even_mask) * f64(odd_weights), 0, "e4m3")
    skip = mxq(f64(llr), 1, "e4m3") @ mxq(f64(w_skipconn2even_mask) * f64(llr_weights), 0, "e4m3")
    pre = np.clip(msgs + skip, -CLIP_TANH, CLIP_TANH)
    return np.tanh(0.5 * pre)

@@ -1,0 +1,241 @@
+from contextlib import ExitStack
+
+import concourse.masks as masks
+import concourse.mybir as mybir
+
+F32 = mybir.dt.float32
+BF16 = mybir.dt.bfloat16
+U32 = mybir.dt.uint32
+U8 = mybir.dt.uint8
+FP8X4 = mybir.dt.float8_e4m3fn_x4
+ALU = mybir.AluOpType
+ACT = mybir.ActivationFunctionType
+
+P = 128
+B = 512
+E = 2048
+N = 1024
+KP = 512
+NPASS = (E + N) // KP
+MT = B // P
+CT = 512
+FLOPS = 2 * B * (E + N) * E
+
+PINNED = True
+NFULL = 0
+RAW_BUFS = 5
+GRP_BUFS = 4
+K_TH = 2
+K_CL = 1
+S_COLS = 384
+S_COLS_BY_UNIT = {}
+TANH5 = 0.9999092042625951
+
+
+def tile_oddlayer_kernel(tc, x, llr, odd_weights, llr_weights, w_odd2even_mask, w_skipconn2even_mask, out):
+    nc = tc.nc
+    with ExitStack() as ctx:
+        if PINNED:
+            ctx.enter_context(tc.manual_schedule())
+        const = ctx.enter_context(tc.tile_pool(name="const", bufs=1))
+        rawp = ctx.enter_context(tc.tile_pool(name="rawp", bufs=RAW_BUFS))
+        grpp = ctx.enter_context(tc.tile_pool(name="grpp", bufs=GRP_BUFS))
+        xgp = ctx.enter_context(tc.tile_pool(name="xgp", bufs=2))
+        psum = ctx.enter_context(tc.psum_pool(name="psum", bufs=1))
+
+        ident = const.tile([P, P], F32, name="ident")
+        masks.make_identity(nc, ident[:])
+        warm = const.tile([P, 2], F32, name="warm")
+        nc.vector.memset(warm[:, 0:1], 0.0)
+        nc.scalar.activation(out=warm[:, 1:2], in_=warm[:, 0:1], func=ACT.Tanh)
+
+        xw = const.tile([P, MT, NPASS * P], U32, name="xw", align_bytes=64)
+        xs = const.tile([P, MT, NPASS * P], U8, name="xs", align_bytes=64)
+        n_units = NPASS * (E // CT)
+        ww = const.tile([P, n_units, CT], U32, name="ww", align_bytes=64)
+        ws = const.tile([P, n_units, CT], U8, name="ws", align_bytes=64)
+        ost = const.tile([P, MT, E], F32, name="ost")
+
+        jobs = []
+        for g in range(NFULL):
+            jobs.append((g, 0, E))
+        for g in range(NFULL, NPASS):
+            jobs.append((g, 0, 2 * CT))
+        for g in range(NFULL, NPASS - 1):
+            jobs.append((g, 2 * CT, 2 * CT))
+        jobs.append((NPASS - 1, 2 * CT, CT))
+        jobs.append((NPASS - 1, 3 * CT, CT))
+
+        state = {"avail": RAW_BUFS, "next": 0}
+        loaded = {}
+
+        def pump():
+            while state["next"] < len(jobs):
+                g, c0, cw = jobs[state["next"]]
+                slots = 2 if cw == E else 1
+                if state["avail"] < slots:
+                    return
+                state["avail"] -= slots
+                wsrc, msrc, r0 = (odd_weights, w_odd2even_mask, g * KP) if g * KP < E else (llr_weights, w_skipconn2even_mask, g * KP - E)
+                if slots == 2:
+                    wt = rawp.tile([P, 4 * E], BF16, tag="raw", name="wt%d" % state["next"])
+                    mt = rawp.tile([P, 4 * E], BF16, tag="raw", name="mt%d" % state["next"])
+                    wv = wt[:].rearrange("p (j c) -> p j c", j=4)
+                    mv = mt[:].rearrange("p (j c) -> p j c", j=4)
+                else:
+                    rt = rawp.tile([P, 4 * E], BF16, tag="raw", name="rt%d" % state["next"])
+                    wv = rt[:, 0:4 * cw].rearrange("p (j c) -> p j c", j=4)
+                    mv = rt[:, 2 * E:2 * E + 4 * cw].rearrange("p (j c) -> p j c", j=4)
+                nc.sync.dma_start(out=wv, in_=wsrc[r0:r0 + KP, c0:c0 + cw].rearrange("(p j) c -> p j c", j=4))
+                nc.sync.dma_start(out=mv, in_=msrc[r0:r0 + KP, c0:c0 + cw].rearrange("(p j) c -> p j c", j=4))
+                loaded[state["next"]] = (wv, mv)
+                state["next"] += 1
+
+        xt = rawp.tile([P, 4 * E], BF16, tag="raw", name="xt")
+        lt = rawp.tile([P, 4 * E], BF16, tag="raw", name="lt")
+        state["avail"] -= 2
+        for m in range(MT):
+            nc.sync.dma_start(out=xt[:, m * E:(m + 1) * E], in_=x[m * P:(m + 1) * P, :])
+        nc.sync.dma_start(out=lt[:, 0:MT * N].rearrange("p (m k) -> p m k", m=MT), in_=llr.rearrange("(m p) k -> p m k", p=P))
+        pump()
+
+        xwords = xt[:].bitcast(F32).rearrange("p (m g w u) -> p m g u w", m=MT, g=E // KP, u=2)
+        lwords = lt[:, 0:MT * N].bitcast(F32).rearrange("p (m g w u) -> p m g u w", m=MT, g=N // KP, u=2)
+        fills = {"n": 0}
+
+        def transposed_bank(words, m, g0):
+            b = fills["n"] % 8
+            pt = psum.tile([P, CT], F32, tag="b%d" % b, name="pt%d" % fills["n"])
+            ptv = pt[:].rearrange("p (g u r) -> p g u r", g=2, u=2)
+            for gg in range(2):
+                for u in range(2):
+                    nc.tensor.transpose(out=ptv[:, gg, u, :], in_=words[:, m, g0 + gg, u, :], identity=ident[:])
+            fills["n"] += 1
+            return ptv.rearrange("p g u r -> p g r u")
+
+        def copy_out(dst, src):
+            if fills["n"] % 2 == 1:
+                nc.vector.tensor_copy(out=dst, in_=src)
+            else:
+                nc.scalar.copy(out=dst, in_=src)
+
+        for m in range(MT):
+            xg = xgp.tile([P, 4 * KP], BF16, tag="xg", name="xg%d" % m, align_bytes=64)
+            xgv = xg[:].bitcast(F32).rearrange("p (g r u) -> p g r u", g=4, u=2)
+            for gp in range(2):
+                src = transposed_bank(xwords, m, 2 * gp)
+                copy_out(xgv[:, 2 * gp:2 * gp + 2, :, :], src)
+            nc.vector.quantize_mx(out=xw[:, m, 0:4 * P].bitcast(FP8X4), scales=xs[:, m, 0:4 * P], in_=xg[:])
+        state["avail"] += 1
+        pump()
+        for m in range(MT):
+            lg = xgp.tile([P, 2 * KP], BF16, tag="lg", name="lg%d" % m, align_bytes=64)
+            lgv = lg[:].bitcast(F32).rearrange("p (g r u) -> p g r u", g=2, u=2)
+            src = transposed_bank(lwords, m, 0)
+            copy_out(lgv, src)
+            nc.vector.quantize_mx(out=xw[:, m, 4 * P:6 * P].bitcast(FP8X4), scales=xs[:, m, 4 * P:6 * P], in_=lg[:])
+        state["avail"] += 1
+        pump()
+
+        units = []
+        for ji, (g, c0, cw) in enumerate(jobs):
+            for a in range(0, cw, CT):
+                units.append((ji, g, (c0 + a) // CT, a, a + CT == cw))
+
+        passes = {}
+        acc = {}
+        th_emitted = set()
+        pe_wait = []
+        bg_th = []
+        bg_cl = []
+        stores = []
+
+        def flush_pe():
+            rest = []
+            blocked = set()
+            for item in pe_wait:
+                ui, g, n, m = item
+                key = (m, n)
+                if key in blocked or (n >= 2 and key not in passes and (m, n - 2) not in th_emitted):
+                    blocked.add(key)
+                    rest.append(item)
+                    continue
+                passes[key] = passes.get(key, 0) + 1
+                if passes[key] == 1:
+                    acc[key] = psum.tile([P, CT], F32, tag="b%d" % (2 * m + n % 2), name="acc%d_%d" % (m, n))
+                nc.tensor.matmul_mx(
+                    out=acc[key][:],
+                    lhsT=xw[:, m, g * P:(g + 1) * P].bitcast(FP8X4),
+                    lhsT_scale=xs[:, m, g * P:(g + 1) * P],
+                    rhs=ww[:, ui, :].bitcast(FP8X4),
+                    rhs_scale=ws[:, ui, :],
+                    start=(passes[key] == 1),
+                    stop=(passes[key] == NPASS),
+                )
+                if passes[key] == NPASS:
+                    bg_th.append(key)
+            pe_wait[:] = rest
+
+        def emit_th(k):
+            todo = bg_th[:k]
+            bg_th[:] = bg_th[k:]
+            for (m, n) in todo:
+                nc.scalar.activation(out=ost[:, m, n * CT:(n + 1) * CT], in_=acc[(m, n)][:], func=ACT.Tanh, scale=0.5)
+                th_emitted.add((m, n))
+                bg_cl.append([m, n, True])
+            if todo:
+                flush_pe()
+
+        def emit_cl(k, fresh_too):
+            done = 0
+            while done < k and bg_cl and (fresh_too or not bg_cl[0][2]):
+                m, n, fresh = bg_cl[0]
+                bg_cl[:] = bg_cl[1:]
+                view = ost[:, m, n * CT:(n + 1) * CT]
+                nc.vector.tensor_scalar(out=view, in0=view, scalar1=TANH5, scalar2=-TANH5, op0=ALU.min, op1=ALU.max)
+                stores.append((m, n))
+                done += 1
+
+        def quantise(ui, gt):
+            ji, g, n, a, last = units[ui]
+            nc.vector.quantize_mx(out=ww[:, ui, :].bitcast(FP8X4), scales=ws[:, ui, :], in_=gt[:])
+            for m in range(MT):
+                pe_wait.append((ui, g, n, m))
+            flush_pe()
+
+        prev = None
+        for ui, (ji, g, n, a, last) in enumerate(units):
+            wv, mv = loaded[ji]
+            full = jobs[ji][2] == E
+            nc.vector.tensor_tensor(out=wv[:, :, a:a + CT], in0=wv[:, :, a:a + CT], in1=mv[:, :, a:a + CT], op=ALU.mult)
+            if full and last:
+                state["avail"] += 1
+            if prev is not None:
+                quantise(prev[0], prev[1])
+            gt = grpp.tile([P, 4 * CT], BF16, tag="g", name="g%d" % ui, align_bytes=64)
+            gv = gt[:].rearrange("p (c t) -> p c t", t=4)
+            cs = S_COLS_BY_UNIT.get(ui, S_COLS)
+            if cs > 0:
+                nc.scalar.copy(
+                    out=gv[:, 0:cs, :].rearrange("p (c i) t -> p c t i", i=4),
+                    in_=wv[:, :, a:a + cs].rearrange("p t (c i) -> p c t i", i=4),
+                )
+            if cs < CT:
+                nc.vector.tensor_copy(
+                    out=gv[:, cs:CT, :].rearrange("p (c i) t -> p c t i", i=4),
+                    in_=wv[:, :, a + cs:a + CT].rearrange("p t (c i) -> p c t i", i=4),
+                )
+            if last:
+                state["avail"] += 1
+            pump()
+            for item in bg_cl:
+                item[2] = False
+            emit_cl(K_CL, False)
+            emit_th(K_TH)
+            prev = (ui, gt)
+        quantise(prev[0], prev[1])
+        while bg_th or pe_wait:
+            emit_th(8)
+        emit_cl(99, True)
+        for (m, n) in stores:
+            nc.sync.dma_start(out=out[m * P:(m + 1) * P, n * CT:(n + 1) * CT], in_=ost[:, m, n * CT:(n + 1) * CT])

@@ -24,8 +24,9 @@ FLOPS = 2 * B * (E + N) * E
 PINNED = True
 NFULL = 0
 RAW_BUFS = 5
-GRP_BUFS = 4
+GRP_BUFS = 5
 K_TH = 2
+Q_LAG = 2
 K_CL = 1
 S_COLS = 384
 S_COLS_BY_UNIT = {}
@@ -203,15 +204,21 @@ def tile_oddlayer_kernel(tc, x, llr, odd_weights, llr_weights, w_odd2even_mask, 
                 pe_wait.append((ui, g, n, m))
             flush_pe()
 
-        prev = None
+        pend = []
         for ui, (ji, g, n, a, last) in enumerate(units):
             wv, mv = loaded[ji]
             full = jobs[ji][2] == E
-            nc.vector.tensor_tensor(out=wv[:, :, a:a + CT], in0=wv[:, :, a:a + CT], in1=mv[:, :, a:a + CT], op=ALU.mult)
-            if full and last:
-                state["avail"] += 1
-            if prev is not None:
-                quantise(prev[0], prev[1])
+            if a == 0:
+                halves = 2 if full else 1
+                for h in range(halves):
+                    j0 = h * (4 // halves)
+                    j1 = j0 + 4 // halves
+                    nc.vector.tensor_tensor(out=wv[:, j0:j1, :], in0=wv[:, j0:j1, :], in1=mv[:, j0:j1, :], op=ALU.mult)
+                if full:
+                    state["avail"] += 1
+            while len(pend) >= Q_LAG:
+                quantise(pend[0][0], pend[0][1])
+                pend[:] = pend[1:]
             gt = grpp.tile([P, 4 * CT], BF16, tag="g", name="g%d" % ui, align_bytes=64)
             gv = gt[:].rearrange("p (c t) -> p c t", t=4)
             cs = S_COLS_BY_UNIT.get(ui, S_COLS)
@@ -232,8 +239,9 @@ def tile_oddlayer_kernel(tc, x, llr, odd_weights, llr_weights, w_odd2even_mask, 
                 item[2] = False
             emit_cl(K_CL, False)
             emit_th(K_TH)
-            prev = (ui, gt)
-        quantise(prev[0], prev[1])
+            pend.append((ui, gt))
+        for (ui, gt) in pend:
+            quantise(ui, gt)
         while bg_th or pe_wait:
             emit_th(8)
         emit_cl(99, True)

@@ -22,14 +22,14 @@ CT = 512
 FLOPS = 2 * B * (E + N) * E
 
 PINNED = True
-NFULL = 0
+NFULL = 2
 RAW_BUFS = 5
 GRP_BUFS = 5
 K_TH = 2
-Q_LAG = 2
+Q_LAG = 1
 K_CL = 1
-S_COLS = 384
-S_COLS_BY_UNIT = {}
+S_COLS = {2048: (0, 256, 384, 512), 1024: (128, 512)}
+S_COLS_TAIL = (384, 256)
 TANH5 = 0.9999092042625951
 
 
@@ -87,17 +87,22 @@ def tile_oddlayer_kernel(tc, x, llr, odd_weights, llr_weights, w_odd2even_mask, 
                     rt = rawp.tile([P, 4 * E], BF16, tag="raw", name="rt%d" % state["next"])
                     wv = rt[:, 0:4 * cw].rearrange("p (j c) -> p j c", j=4)
                     mv = rt[:, 2 * E:2 * E + 4 * cw].rearrange("p (j c) -> p j c", j=4)
-                nc.sync.dma_start(out=wv, in_=wsrc[r0:r0 + KP, c0:c0 + cw].rearrange("(p j) c -> p j c", j=4))
-                nc.sync.dma_start(out=mv, in_=msrc[r0:r0 + KP, c0:c0 + cw].rearrange("(p j) c -> p j c", j=4))
+                wrows = wsrc[r0:r0 + KP, c0:c0 + cw].rearrange("(p j) c -> p j c", j=4)
+                mrows = msrc[r0:r0 + KP, c0:c0 + cw].rearrange("(p j) c -> p j c", j=4)
+                for j0 in range(0, 4, 4 // slots):
+                    j1 = j0 + 4 // slots
+                    nc.sync.dma_start(out=wv[:, j0:j1, :], in_=wrows[:, j0:j1, :])
+                    nc.sync.dma_start(out=mv[:, j0:j1, :], in_=mrows[:, j0:j1, :])
                 loaded[state["next"]] = (wv, mv)
                 state["next"] += 1
 
         xt = rawp.tile([P, 4 * E], BF16, tag="raw", name="xt")
         lt = rawp.tile([P, 4 * E], BF16, tag="raw", name="lt")
         state["avail"] -= 2
-        for m in range(MT):
-            nc.sync.dma_start(out=xt[:, m * E:(m + 1) * E], in_=x[m * P:(m + 1) * P, :])
-        nc.sync.dma_start(out=lt[:, 0:MT * N].rearrange("p (m k) -> p m k", m=MT), in_=llr.rearrange("(m p) k -> p m k", p=P))
+        xrows = x.rearrange("(p m) k -> p m k", m=MT)
+        for m in range(0, MT, 2):
+            nc.sync.dma_start(out=xt[:, m * E:(m + 2) * E].rearrange("p (m k) -> p m k", m=2), in_=xrows[:, m:m + 2, :])
+        nc.sync.dma_start(out=lt[:, 0:MT * N].rearrange("p (m k) -> p m k", m=MT), in_=llr.rearrange("(p m) k -> p m k", m=MT))
         pump()
 
         xwords = xt[:].bitcast(F32).rearrange("p (m g w u) -> p m g u w", m=MT, g=E // KP, u=2)
@@ -221,7 +226,10 @@ def tile_oddlayer_kernel(tc, x, llr, odd_weights, llr_weights, w_odd2even_mask, 
                 pend[:] = pend[1:]
             gt = grpp.tile([P, 4 * CT], BF16, tag="g", name="g%d" % ui, align_bytes=64)
             gv = gt[:].rearrange("p (c t) -> p c t", t=4)
-            cs = S_COLS_BY_UNIT.get(ui, S_COLS)
+            if ui >= len(units) - len(S_COLS_TAIL):
+                cs = S_COLS_TAIL[ui - (len(units) - len(S_COLS_TAIL))]
+            else:
+                cs = S_COLS[jobs[ji][2]][a // CT]
             if cs > 0:
                 nc.scalar.copy(
                     out=gv[:, 0:cs, :].rearrange("p (c i) t -> p c t i", i=4),
@@ -238,12 +246,16 @@ def tile_oddlayer_kernel(tc, x, llr, odd_weights, llr_weights, w_odd2even_mask, 
             for item in bg_cl:
                 item[2] = False
             emit_cl(K_CL, False)
-            emit_th(K_TH)
+            emit_th(8 if ui >= len(units) - 4 else K_TH)
             pend.append((ui, gt))
         for (ui, gt) in pend:
             quantise(ui, gt)
         while bg_th or pe_wait:
             emit_th(8)
         emit_cl(99, True)
+        orows = out.rearrange("(p m) c -> p m c", m=MT)
+        for m in range(MT):
+            nc.sync.dma_start(out=orows[:, m, 0:2 * CT], in_=ost[:, m, 0:2 * CT])
         for (m, n) in stores:
-            nc.sync.dma_start(out=out[m * P:(m + 1) * P, n * CT:(n + 1) * CT], in_=ost[:, m, n * CT:(n + 1) * CT])
+            if n >= 2:
+                nc.sync.dma_start(out=orows[:, m, n * CT:(n + 1) * CT], in_=ost[:, m, n * CT:(n + 1) * CT])

@@ -26,10 +26,11 @@ NFULL = 2
 RAW_BUFS = 5
 GRP_BUFS = 5
 K_TH = 2
-Q_LAG = 1
-K_CL = 1
-S_COLS = {2048: (0, 256, 384, 512), 1024: (128, 512)}
-S_COLS_TAIL = (384, 256)
+Q_LAG = 2
+K_CL = 2
+CL_LAG = 2
+S_COLS = {2048: (384, 384, 384, 384), 1024: (384, 384), 512: (384,)}
+S_COLS_TAIL = (192,)
 TANH5 = 0.9999092042625951
 
 
@@ -62,10 +63,11 @@ def tile_oddlayer_kernel(tc, x, llr, odd_weights, llr_weights, w_odd2even_mask, 
             jobs.append((g, 0, E))
         for g in range(NFULL, NPASS):
             jobs.append((g, 0, 2 * CT))
-        for g in range(NFULL, NPASS - 1):
+        for g in range(NFULL, NPASS - 2):
             jobs.append((g, 2 * CT, 2 * CT))
-        jobs.append((NPASS - 1, 2 * CT, CT))
-        jobs.append((NPASS - 1, 3 * CT, CT))
+        for n in (2, 3):
+            for g in (NPASS - 2, NPASS - 1):
+                jobs.append((g, n * CT, CT))
 
         state = {"avail": RAW_BUFS, "next": 0}
         loaded = {}
@@ -188,14 +190,14 @@ def tile_oddlayer_kernel(tc, x, llr, odd_weights, llr_weights, w_odd2even_mask, 
             for (m, n) in todo:
                 nc.scalar.activation(out=ost[:, m, n * CT:(n + 1) * CT], in_=acc[(m, n)][:], func=ACT.Tanh, scale=0.5)
                 th_emitted.add((m, n))
-                bg_cl.append([m, n, True])
+                bg_cl.append([m, n, 0])
             if todo:
                 flush_pe()
 
-        def emit_cl(k, fresh_too):
+        def emit_cl(k, min_age):
             done = 0
-            while done < k and bg_cl and (fresh_too or not bg_cl[0][2]):
-                m, n, fresh = bg_cl[0]
+            while done < k and bg_cl and bg_cl[0][2] >= min_age:
+                m, n, age = bg_cl[0]
                 bg_cl[:] = bg_cl[1:]
                 view = ost[:, m, n * CT:(n + 1) * CT]
                 nc.vector.tensor_scalar(out=view, in0=view, scalar1=TANH5, scalar2=-TANH5, op0=ALU.min, op1=ALU.max)
@@ -244,15 +246,15 @@ def tile_oddlayer_kernel(tc, x, llr, odd_weights, llr_weights, w_odd2even_mask, 
                 state["avail"] += 1
             pump()
             for item in bg_cl:
-                item[2] = False
-            emit_cl(K_CL, False)
+                item[2] += 1
+            emit_cl(K_CL, CL_LAG)
             emit_th(8 if ui >= len(units) - 4 else K_TH)
             pend.append((ui, gt))
         for (ui, gt) in pend:
             quantise(ui, gt)
         while bg_th or pe_wait:
             emit_th(8)
-        emit_cl(99, True)
+        emit_cl(99, 0)
         orows = out.rearrange("(p m) c -> p m c", m=MT)
         for m in range(MT):
             nc.sync.dma_start(out=orows[:, m, 0:2 * CT], in_=ost[:, m, 0:2 * CT])

@@ -21,24 +21,30 @@ MT = B // P
 CT = 512
 FLOPS = 2 * B * (E + N) * E
 
-PINNED = True
+FULL_PARTS = 2
 NFULL = 2
+NWIDE = 5
 RAW_BUFS = 5
 GRP_BUFS = 5
 K_TH = 2
 Q_LAG = 2
+N_END = 4
 K_CL = 2
 CL_LAG = 2
-S_COLS = {2048: (384, 384, 384, 384), 1024: (384, 384), 512: (384,)}
-S_COLS_TAIL = (192,)
+S_COLS = 352
+S_COLS_T1 = 320
+S_COLS_LATE = 384
+T1_JOBS = (6,)
+SPLIT_HALF = 1
+X_ON_S = 0
+S_COLS_TAIL = (256,)
 TANH5 = 0.9999092042625951
 
 
 def tile_oddlayer_kernel(tc, x, llr, odd_weights, llr_weights, w_odd2even_mask, w_skipconn2even_mask, out):
     nc = tc.nc
     with ExitStack() as ctx:
-        if PINNED:
-            ctx.enter_context(tc.manual_schedule())
+        ctx.enter_context(tc.manual_schedule())
         const = ctx.enter_context(tc.tile_pool(name="const", bufs=1))
         rawp = ctx.enter_context(tc.tile_pool(name="rawp", bufs=RAW_BUFS))
         grpp = ctx.enter_context(tc.tile_pool(name="grpp", bufs=GRP_BUFS))
@@ -61,21 +67,27 @@ def tile_oddlayer_kernel(tc, x, llr, odd_weights, llr_weights, w_odd2even_mask, 
         jobs = []
         for g in range(NFULL):
             jobs.append((g, 0, E))
-        for g in range(NFULL, NPASS):
+        for g in range(NFULL, NWIDE):
             jobs.append((g, 0, 2 * CT))
-        for g in range(NFULL, NPASS - 2):
+        for g in range(NWIDE, NPASS):
+            jobs.append((g, 0, 3 * CT))
+        for g in range(NFULL, NWIDE):
             jobs.append((g, 2 * CT, 2 * CT))
-        for n in (2, 3):
-            for g in (NPASS - 2, NPASS - 1):
-                jobs.append((g, n * CT, CT))
+        for g in range(NWIDE, NPASS):
+            jobs.append((g, 3 * CT, CT))
 
         state = {"avail": RAW_BUFS, "next": 0}
         loaded = {}
 
+        def parts_of(ji):
+            if jobs[ji][2] > 2 * CT:
+                return 2 if ji == 0 or jobs[ji][2] < E else FULL_PARTS
+            return 2 if jobs[ji][2] == 2 * CT and SPLIT_HALF else 1
+
         def pump():
             while state["next"] < len(jobs):
                 g, c0, cw = jobs[state["next"]]
-                slots = 2 if cw == E else 1
+                slots = 2 if cw > 2 * CT else 1
                 if state["avail"] < slots:
                     return
                 state["avail"] -= slots
@@ -83,16 +95,17 @@ def tile_oddlayer_kernel(tc, x, llr, odd_weights, llr_weights, w_odd2even_mask, 
                 if slots == 2:
                     wt = rawp.tile([P, 4 * E], BF16, tag="raw", name="wt%d" % state["next"])
                     mt = rawp.tile([P, 4 * E], BF16, tag="raw", name="mt%d" % state["next"])
-                    wv = wt[:].rearrange("p (j c) -> p j c", j=4)
-                    mv = mt[:].rearrange("p (j c) -> p j c", j=4)
+                    wv = wt[:, 0:4 * cw].rearrange("p (j c) -> p j c", j=4)
+                    mv = mt[:, 0:4 * cw].rearrange("p (j c) -> p j c", j=4)
                 else:
                     rt = rawp.tile([P, 4 * E], BF16, tag="raw", name="rt%d" % state["next"])
                     wv = rt[:, 0:4 * cw].rearrange("p (j c) -> p j c", j=4)
                     mv = rt[:, 2 * E:2 * E + 4 * cw].rearrange("p (j c) -> p j c", j=4)
                 wrows = wsrc[r0:r0 + KP, c0:c0 + cw].rearrange("(p j) c -> p j c", j=4)
                 mrows = msrc[r0:r0 + KP, c0:c0 + cw].rearrange("(p j) c -> p j c", j=4)
-                for j0 in range(0, 4, 4 // slots):
-                    j1 = j0 + 4 // slots
+                parts = parts_of(state["next"])
+                for h in range(parts):
+                    j0, j1 = h * 4 // parts, (h + 1) * 4 // parts
                     nc.sync.dma_start(out=wv[:, j0:j1, :], in_=wrows[:, j0:j1, :])
                     nc.sync.dma_start(out=mv[:, j0:j1, :], in_=mrows[:, j0:j1, :])
                 loaded[state["next"]] = (wv, mv)
@@ -122,7 +135,7 @@ def tile_oddlayer_kernel(tc, x, llr, odd_weights, llr_weights, w_odd2even_mask, 
             return ptv.rearrange("p g u r -> p g r u")
 
         def copy_out(dst, src):
-            if fills["n"] % 2 == 1:
+            if fills["n"] % 2 == 1 and not X_ON_S:
                 nc.vector.tensor_copy(out=dst, in_=src)
             else:
                 nc.scalar.copy(out=dst, in_=src)
@@ -190,18 +203,21 @@ def tile_oddlayer_kernel(tc, x, llr, odd_weights, llr_weights, w_odd2even_mask, 
             for (m, n) in todo:
                 nc.scalar.activation(out=ost[:, m, n * CT:(n + 1) * CT], in_=acc[(m, n)][:], func=ACT.Tanh, scale=0.5)
                 th_emitted.add((m, n))
-                bg_cl.append([m, n, 0])
+                if n >= 2:
+                    bg_cl.append([m, n * CT, CT, 0])
+                elif (m, 1 - n) in th_emitted:
+                    bg_cl.append([m, 0, 2 * CT, 0])
             if todo:
                 flush_pe()
 
         def emit_cl(k, min_age):
             done = 0
-            while done < k and bg_cl and bg_cl[0][2] >= min_age:
-                m, n, age = bg_cl[0]
+            while done < k and bg_cl and bg_cl[0][3] >= min_age:
+                m, c0, cw, age = bg_cl[0]
                 bg_cl[:] = bg_cl[1:]
-                view = ost[:, m, n * CT:(n + 1) * CT]
+                view = ost[:, m, c0:c0 + cw]
                 nc.vector.tensor_scalar(out=view, in0=view, scalar1=TANH5, scalar2=-TANH5, op0=ALU.min, op1=ALU.max)
-                stores.append((m, n))
+                stores.append((m, c0, cw))
                 done += 1
 
         def quantise(ui, gt):
@@ -214,9 +230,9 @@ def tile_oddlayer_kernel(tc, x, llr, odd_weights, llr_weights, w_odd2even_mask, 
         pend = []
         for ui, (ji, g, n, a, last) in enumerate(units):
             wv, mv = loaded[ji]
-            full = jobs[ji][2] == E
+            full = jobs[ji][2] > 2 * CT
             if a == 0:
-                halves = 2 if full else 1
+                halves = 2 if full else parts_of(ji)
                 for h in range(halves):
                     j0 = h * (4 // halves)
                     j1 = j0 + 4 // halves
@@ -231,7 +247,7 @@ def tile_oddlayer_kernel(tc, x, llr, odd_weights, llr_weights, w_odd2even_mask, 
             if ui >= len(units) - len(S_COLS_TAIL):
                 cs = S_COLS_TAIL[ui - (len(units) - len(S_COLS_TAIL))]
             else:
-                cs = S_COLS[jobs[ji][2]][a // CT]
+                cs = S_COLS_T1 if ji in T1_JOBS else S_COLS_LATE if jobs[ji][1] > 0 else S_COLS
             if cs > 0:
                 nc.scalar.copy(
                     out=gv[:, 0:cs, :].rearrange("p (c i) t -> p c t i", i=4),
@@ -246,9 +262,9 @@ def tile_oddlayer_kernel(tc, x, llr, odd_weights, llr_weights, w_odd2even_mask, 
                 state["avail"] += 1
             pump()
             for item in bg_cl:
-                item[2] += 1
+                item[3] += 1
             emit_cl(K_CL, CL_LAG)
-            emit_th(8 if ui >= len(units) - 4 else K_TH)
+            emit_th(8 if ui >= len(units) - N_END else K_TH)
             pend.append((ui, gt))
         for (ui, gt) in pend:
             quantise(ui, gt)
@@ -256,8 +272,5 @@ def tile_oddlayer_kernel(tc, x, llr, odd_weights, llr_weights, w_odd2even_mask, 
             emit_th(8)
         emit_cl(99, 0)
         orows = out.rearrange("(p m) c -> p m c", m=MT)
-        for m in range(MT):
-            nc.sync.dma_start(out=orows[:, m, 0:2 * CT], in_=ost[:, m, 0:2 * CT])
-        for (m, n) in stores:
-            if n >= 2:
-                nc.sync.dma_start(out=orows[:, m, n * CT:(n + 1) * CT], in_=ost[:, m, n * CT:(n + 1) * CT])
+        for (m, c0, cw) in stores:
+            nc.sync.dma_start(out=orows[:, m, c0:c0 + cw], in_=ost[:, m, c0:c0 + cw])

@@ -250,13 +250,13 @@ def tile_oddlayer_kernel(tc, x, llr, odd_weights, llr_weights, w_odd2even_mask, 
                 cs = S_COLS_T1 if ji in T1_JOBS else S_COLS_LATE if jobs[ji][1] > 0 else S_COLS
             if cs > 0:
                 nc.scalar.copy(
-                    out=gv[:, 0:cs, :].rearrange("p (c i) t -> p c t i", i=4),
-                    in_=wv[:, :, a:a + cs].rearrange("p t (c i) -> p c t i", i=4),
+                    out=gv[:, 0:cs, :].rearrange("p (c i) t -> p c t i", i=8),
+                    in_=wv[:, :, a:a + cs].rearrange("p t (c i) -> p c t i", i=8),
                 )
             if cs < CT:
                 nc.vector.tensor_copy(
-                    out=gv[:, cs:CT, :].rearrange("p (c i) t -> p c t i", i=4),
-                    in_=wv[:, :, a + cs:a + CT].rearrange("p t (c i) -> p c t i", i=4),
+                    out=gv[:, cs:CT, :].rearrange("p (c i) t -> p c t i", i=8),
+                    in_=wv[:, :, a + cs:a + CT].rearrange("p t (c i) -> p c t i", i=8),
                 )
             if last:
                 state["avail"] += 1

from contextlib import ExitStack

import concourse.masks as masks
import concourse.mybir as mybir

F32 = mybir.dt.float32
BF16 = mybir.dt.bfloat16
U32 = mybir.dt.uint32
U8 = mybir.dt.uint8
FP8X4 = mybir.dt.float8_e4m3fn_x4
ALU = mybir.AluOpType
ACT = mybir.ActivationFunctionType

P = 128
B = 512
E = 2048
N = 1024
KP = 512
NPASS = (E + N) // KP
MT = B // P
CT = 512
FLOPS = 2 * B * (E + N) * E

FULL_PARTS = 2
NFULL = 2
NWIDE = 5
RAW_BUFS = 5
GRP_BUFS = 5
K_TH = 2
Q_LAG = 2
N_END = 4
K_CL = 2
CL_LAG = 2
S_COLS = 352
S_COLS_T1 = 320
S_COLS_LATE = 384
T1_JOBS = (6,)
SPLIT_HALF = 1
X_ON_S = 0
S_COLS_TAIL = (256,)
TANH5 = 0.9999092042625951


def tile_oddlayer_kernel(tc, x, llr, odd_weights, llr_weights, w_odd2even_mask, w_skipconn2even_mask, out):
    nc = tc.nc
    with ExitStack() as ctx:
        ctx.enter_context(tc.manual_schedule())
        const = ctx.enter_context(tc.tile_pool(name="const", bufs=1))
        rawp = ctx.enter_context(tc.tile_pool(name="rawp", bufs=RAW_BUFS))
        grpp = ctx.enter_context(tc.tile_pool(name="grpp", bufs=GRP_BUFS))
        xgp = ctx.enter_context(tc.tile_pool(name="xgp", bufs=2))
        psum = ctx.enter_context(tc.psum_pool(name="psum", bufs=1))

        ident = const.tile([P, P], F32, name="ident")
        masks.make_identity(nc, ident[:])
        warm = const.tile([P, 2], F32, name="warm")
        nc.vector.memset(warm[:, 0:1], 0.0)
        nc.scalar.activation(out=warm[:, 1:2], in_=warm[:, 0:1], func=ACT.Tanh)

        xw = const.tile([P, MT, NPASS * P], U32, name="xw", align_bytes=64)
        xs = const.tile([P, MT, NPASS * P], U8, name="xs", align_bytes=64)
        n_units = NPASS * (E // CT)
        ww = const.tile([P, n_units, CT], U32, name="ww", align_bytes=64)
        ws = const.tile([P, n_units, CT], U8, name="ws", align_bytes=64)
        ost = const.tile([P, MT, E], F32, name="ost")

        jobs = []
        for g in range(NFULL):
            jobs.append((g, 0, E))
        for g in range(NFULL, NWIDE):
            jobs.append((g, 0, 2 * CT))
        for g in range(NWIDE, NPASS):
            jobs.append((g, 0, 3 * CT))
        for g in range(NFULL, NWIDE):
            jobs.append((g, 2 * CT, 2 * CT))
        for g in range(NWIDE, NPASS):
            jobs.append((g, 3 * CT, CT))

        state = {"avail": RAW_BUFS, "next": 0}
        loaded = {}

        def parts_of(ji):
            if jobs[ji][2] > 2 * CT:
                return 2 if ji == 0 or jobs[ji][2] < E else FULL_PARTS
            return 2 if jobs[ji][2] == 2 * CT and SPLIT_HALF else 1

        def pump():
            while state["next"] < len(jobs):
                g, c0, cw = jobs[state["next"]]
                slots = 2 if cw > 2 * CT else 1
                if state["avail"] < slots:
                    return
                state["avail"] -= slots
                wsrc, msrc, r0 = (odd_weights, w_odd2even_mask, g * KP) if g * KP < E else (llr_weights, w_skipconn2even_mask, g * KP - E)
                if slots == 2:
                    wt = rawp.tile([P, 4 * E], BF16, tag="raw", name="wt%d" % state["next"])
                    mt = rawp.tile([P, 4 * E], BF16, tag="raw", name="mt%d" % state["next"])
                    wv = wt[:, 0:4 * cw].rearrange("p (j c) -> p j c", j=4)
                    mv = mt[:, 0:4 * cw].rearrange("p (j c) -> p j c", j=4)
                else:
                    rt = rawp.tile([P, 4 * E], BF16, tag="raw", name="rt%d" % state["next"])
                    wv = rt[:, 0:4 * cw].rearrange("p (j c) -> p j c", j=4)
                    mv = rt[:, 2 * E:2 * E + 4 * cw].rearrange("p (j c) -> p j c", j=4)
                wrows = wsrc[r0:r0 + KP, c0:c0 + cw].rearrange("(p j) c -> p j c", j=4)
                mrows = msrc[r0:r0 + KP, c0:c0 + cw].rearrange("(p j) c -> p j c", j=4)
                parts = parts_of(state["next"])
                for h in range(parts):
                    j0, j1 = h * 4 // parts, (h + 1) * 4 // parts
                    nc.sync.dma_start(out=wv[:, j0:j1, :], in_=wrows[:, j0:j1, :])
                    nc.sync.dma_start(out=mv[:, j0:j1, :], in_=mrows[:, j0:j1, :])
                loaded[state["next"]] = (wv, mv)
                state["next"] += 1

        xt = rawp.tile([P, 4 * E], BF16, tag="raw", name="xt")
        lt = rawp.tile([P, 4 * E], BF16, tag="raw", name="lt")
        state["avail"] -= 2
        xrows = x.rearrange("(p m) k -> p m k", m=MT)
        for m in range(0, MT, 2):
            nc.sync.dma_start(out=xt[:, m * E:(m + 2) * E].rearrange("p (m k) -> p m k", m=2), in_=xrows[:, m:m + 2, :])
        nc.sync.dma_start(out=lt[:, 0:MT * N].rearrange("p (m k) -> p m k", m=MT), in_=llr.rearrange("(p m) k -> p m k", m=MT))
        pump()

        xwords = xt[:].bitcast(F32).rearrange("p (m g w u) -> p m g u w", m=MT, g=E // KP, u=2)
        lwords = lt[:, 0:MT * N].bitcast(F32).rearrange("p (m g w u) -> p m g u w", m=MT, g=N // KP, u=2)
        fills = {"n": 0}

        def transposed_bank(words, m, g0):
            b = fills["n"] % 8
            pt = psum.tile([P, CT], F32, tag="b%d" % b, name="pt%d" % fills["n"])
            ptv = pt[:].rearrange("p (g u r) -> p g u r", g=2, u=2)
            for gg in range(2):
                for u in range(2):
                    nc.tensor.transpose(out=ptv[:, gg, u, :], in_=words[:, m, g0 + gg, u, :], identity=ident[:])
            fills["n"] += 1
            return ptv.rearrange("p g u r -> p g r u")

        def copy_out(dst, src):
            if fills["n"] % 2 == 1 and not X_ON_S:
                nc.vector.tensor_copy(out=dst, in_=src)
            else:
                nc.scalar.copy(out=dst, in_=src)

        for m in range(MT):
            xg = xgp.tile([P, 4 * KP], BF16, tag="xg", name="xg%d" % m, align_bytes=64)
            xgv = xg[:].bitcast(F32).rearrange("p (g r u) -> p g r u", g=4, u=2)
            for gp in range(2):
                src = transposed_bank(xwords, m, 2 * gp)
                copy_out(xgv[:, 2 * gp:2 * gp + 2, :, :], src)
            nc.vector.quantize_mx(out=xw[:, m, 0:4 * P].bitcast(FP8X4), scales=xs[:, m, 0:4 * P], in_=xg[:])
        state["avail"] += 1
        pump()
        for m in range(MT):
            lg = xgp.tile([P, 2 * KP], BF16, tag="lg", name="lg%d" % m, align_bytes=64)
            lgv = lg[:].bitcast(F32).rearrange("p (g r u) -> p g r u", g=2, u=2)
            src = transposed_bank(lwords, m, 0)
            copy_out(lgv, src)
            nc.vector.quantize_mx(out=xw[:, m, 4 * P:6 * P].bitcast(FP8X4), scales=xs[:, m, 4 * P:6 * P], in_=lg[:])
        state["avail"] += 1
        pump()

        units = []
        for ji, (g, c0, cw) in enumerate(jobs):
            for a in range(0, cw, CT):
                units.append((ji, g, (c0 + a) // CT, a, a + CT == cw))

        passes = {}
        acc = {}
        th_emitted = set()
        pe_wait = []
        bg_th = []
        bg_cl = []
        stores = []

        def flush_pe():
            rest = []
            blocked = set()
            for item in pe_wait:
                ui, g, n, m = item
                key = (m, n)
                if key in blocked or (n >= 2 and key not in passes and (m, n - 2) not in th_emitted):
                    blocked.add(key)
                    rest.append(item)
                    continue
                passes[key] = passes.get(key, 0) + 1
                if passes[key] == 1:
                    acc[key] = psum.tile([P, CT], F32, tag="b%d" % (2 * m + n % 2), name="acc%d_%d" % (m, n))
                nc.tensor.matmul_mx(
                    out=acc[key][:],
                    lhsT=xw[:, m, g * P:(g + 1) * P].bitcast(FP8X4),
                    lhsT_scale=xs[:, m, g * P:(g + 1) * P],
                    rhs=ww[:, ui, :].bitcast(FP8X4),
                    rhs_scale=ws[:, ui, :],
                    start=(passes[key] == 1),
                    stop=(passes[key] == NPASS),
                )
                if passes[key] == NPASS:
                    bg_th.append(key)
            pe_wait[:] = rest

        def emit_th(k):
            todo = bg_th[:k]
            bg_th[:] = bg_th[k:]
            for (m, n) in todo:
                nc.scalar.activation(out=ost[:, m, n * CT:(n + 1) * CT], in_=acc[(m, n)][:], func=ACT.Tanh, scale=0.5)
                th_emitted.add((m, n))
                if n >= 2:
                    bg_cl.append([m, n * CT, CT, 0])
                elif (m, 1 - n) in th_emitted:
                    bg_cl.append([m, 0, 2 * CT, 0])
            if todo:
                flush_pe()

        def emit_cl(k, min_age):
            done = 0
            while done < k and bg_cl and bg_cl[0][3] >= min_age:
                m, c0, cw, age = bg_cl[0]
                bg_cl[:] = bg_cl[1:]
                view = ost[:, m, c0:c0 + cw]
                nc.vector.tensor_scalar(out=view, in0=view, scalar1=TANH5, scalar2=-TANH5, op0=ALU.min, op1=ALU.max)
                stores.append((m, c0, cw))
                done += 1

        def quantise(ui, gt):
            ji, g, n, a, last = units[ui]
            nc.vector.quantize_mx(out=ww[:, ui, :].bitcast(FP8X4), scales=ws[:, ui, :], in_=gt[:])
            for m in range(MT):
                pe_wait.append((ui, g, n, m))
            flush_pe()

        pend = []
        for ui, (ji, g, n, a, last) in enumerate(units):
            wv, mv = loaded[ji]
            full = jobs[ji][2] > 2 * CT
            if a == 0:
                halves = 2 if full else parts_of(ji)
                for h in range(halves):
                    j0 = h * (4 // halves)
                    j1 = j0 + 4 // halves
                    nc.vector.tensor_tensor(out=wv[:, j0:j1, :], in0=wv[:, j0:j1, :], in1=mv[:, j0:j1, :], op=ALU.mult)
                if full:
                    state["avail"] += 1
            while len(pend) >= Q_LAG:
                quantise(pend[0][0], pend[0][1])
                pend[:] = pend[1:]
            gt = grpp.tile([P, 4 * CT], BF16, tag="g", name="g%d" % ui, align_bytes=64)
            gv = gt[:].rearrange("p (c t) -> p c t", t=4)
            if ui >= len(units) - len(S_COLS_TAIL):
                cs = S_COLS_TAIL[ui - (len(units) - len(S_COLS_TAIL))]
            else:
                cs = S_COLS_T1 if ji in T1_JOBS else S_COLS_LATE if jobs[ji][1] > 0 else S_COLS
            if cs > 0:
                nc.scalar.copy(
                    out=gv[:, 0:cs, :].rearrange("p (c i) t -> p c t i", i=8),
                    in_=wv[:, :, a:a + cs].rearrange("p t (c i) -> p c t i", i=8),
                )
            if cs < CT:
                nc.vector.tensor_copy(
                    out=gv[:, cs:CT, :].rearrange("p (c i) t -> p c t i", i=8),
                    in_=wv[:, :, a + cs:a + CT].rearrange("p t (c i) -> p c t i", i=8),
                )
            if last:
                state["avail"] += 1
            pump()
            for item in bg_cl:
                item[3] += 1
            emit_cl(K_CL, CL_LAG)
            emit_th(8 if ui >= len(units) - N_END else K_TH)
            pend.append((ui, gt))
        for (ui, gt) in pend:
            quantise(ui, gt)
        while bg_th or pe_wait:
            emit_th(8)
        emit_cl(99, 0)
        orows = out.rearrange("(p m) c -> p m c", m=MT)
        for (m, c0, cw) in stores:
            nc.sync.dma_start(out=orows[:, m, c0:c0 + cw], in_=ost[:, m, c0:c0 + cw])
